import numpy as np
import ml_dtypes


def mxq(x, axis, fmt="e4m3"):
    dtype, down = {"e4m3": (ml_dtypes.float8_e4m3fn, 7), "e5m2": (ml_dtypes.float8_e5m2, 14)}[fmt]
    v = np.moveaxis(np.asarray(x, np.float32).astype(ml_dtypes.bfloat16).astype(np.float64), axis, -1)
    blocks = v.reshape(v.shape[:-1] + (-1, 32))
    amax = np.abs(blocks).max(-1, keepdims=True)
    byte = np.maximum(np.where(amax > 0, np.frexp(amax)[1] - 1 + 127, 0) - down, 1)
    scale = np.exp2(byte - 127.0)
    codes = (blocks / scale).astype(np.float32).astype(dtype).astype(np.float64)
    return np.moveaxis((codes * scale).reshape(v.shape), -1, axis)


WIDE = False


def mx_kscale(k):
    if not WIDE:
        return np.ones(k)
    levels = np.array([10, -10, 5, -5, 0])
    a = np.random.permutation(np.resize(levels, k // 512 * 4)).reshape(k // 512, 4)
    idx = np.arange(k)
    return np.exp2(a[idx // 512, idx % 128 // 32])


BF16 = ml_dtypes.bfloat16


def bf(x):
    return np.asarray(x, np.float32).astype(BF16)


def f64(x):
    return np.asarray(x).astype(np.float64)


E2M1 = np.array([0.0, 0.5, 1.0, 1.5, 2.0, 3.0, 4.0, 6.0, -0.0, -0.5, -1.0, -1.5, -2.0, -3.0, -4.0, -6.0])


def pack_weight(w, fmt):
    k, n = w.shape
    w = f64(bf(w)).reshape(k // 32, 32, n)
    amax = np.abs(w).max(1)
    if fmt == "e4m3":
        byte = np.frexp(amax)[1] - 1 + 127 - 7
    else:
        mant, ex = np.frexp(amax / 6.0)
        byte = np.where(mant > 0.5, ex, ex - 1) + 127
    byte = np.clip(np.where(amax > 0, byte, 1), 1, 254)
    scaled = (w * np.exp2(127.0 - byte)[:, None, :]).reshape(k, n).astype(np.float32)
    by_word = np.ascontiguousarray(scaled.reshape(k // 512, 128, 4, n).transpose(0, 1, 3, 2))
    if fmt == "e4m3":
        words = by_word.astype(ml_dtypes.float8_e4m3fn).view(np.uint8)
    else:
        c = by_word.astype(ml_dtypes.float4_e2m1fn).view(np.uint8) & 0xF
        words = c[..., 0::2] | (c[..., 1::2] << 4)
    return np.ascontiguousarray(words), np.ascontiguousarray(byte.astype(np.uint8).reshape(k // 512, 16, n))


def unpack_weight(words, scales, fmt):
    g, p, n, _ = words.shape
    if fmt == "e4m3":
        vals = np.ascontiguousarray(words).view(ml_dtypes.float8_e4m3fn).astype(np.float64)
    else:
        nib = np.empty((g, p, n, 4), np.uint8)
        nib[..., 0::2] = words & 0xF
        nib[..., 1::2] = words >> 4
        vals = E2M1[nib]
    vals = vals * np.repeat(np.exp2(scales.astype(np.float64) - 127.0), 8, axis=1)[..., None]
    return vals.transpose(0, 1, 3, 2).reshape(g * 512, n)


B, C, K, BK, BN = 128, 4096, 4096, 1, 16
KEEP = 0.3
FMT = "e4m3"


def setup_inputs():
    s = mx_kscale(C)
    x = np.random.standard_normal((B, C)) * s
    weight = np.random.uniform(-1.0, 1.0, (K, C)) * 3.2 / np.sqrt(C)
    blk = (np.random.uniform(0.0, 1.0, (K // BK, C // BN)) < KEEP).astype(np.float64)
    mask = np.repeat(np.repeat(blk, BK, axis=0), BN, axis=1)
    weight = weight * mask / s[None, :]
    bias = np.random.uniform(-1.0, 1.0, K) * 0.5
    words, scales = pack_weight(np.ascontiguousarray(weight.T), FMT)
    return {"x": bf(x), "weight_words": words, "weight_scales": scales, "bias": bf(bias)}


def reference(x, weight_words, weight_scales, bias):
    return np.maximum((mxq(f64(x), 1, "e4m3") @ unpack_weight(weight_words, weight_scales, FMT)) + f64(bias), 0.0)

@@ -1,0 +1,151 @@
+from contextlib import ExitStack
+
+import concourse.mybir as mybir
+from concourse.masks import make_identity
+
+BF16 = mybir.dt.bfloat16
+F32 = mybir.dt.float32
+I32 = mybir.dt.int32
+U8 = mybir.dt.uint8
+U32 = mybir.dt.uint32
+FP8X4 = mybir.dt.float8_e4m3fn_x4
+
+P = 128
+PACK = 4
+K_PASS = P * PACK
+K = 4096
+N = 4096
+GROUPS = K // K_PASS
+BANK_COLS = 512
+BANKS = N // BANK_COLS
+PLANES = 4
+QUADRANTS = 4
+LAST_PIECES = 4
+PIECE_COLS = N // LAST_PIECES
+PIECE_BANKS = BANKS // LAST_PIECES
+
+FLOPS = 2 * P * K * N
+
+
+def tile_sparselinearrelu_w_kernel(tc, x, weight_words, weight_scales, bias, out):
+    nc = tc.nc
+    assert tuple(x.shape) == (P, K)
+    assert tuple(weight_words.shape) == (GROUPS, P, N, PACK)
+    assert tuple(weight_scales.shape) == (GROUPS, K_PASS // 32, N)
+
+    with ExitStack() as ctx:
+        keep = ctx.enter_context(tc.tile_pool(name="keep", bufs=1))
+        psum = ctx.enter_context(tc.psum_pool(name="psum", bufs=1))
+        ctx.enter_context(tc.manual_schedule())
+
+        x_sb = keep.tile([P, K], BF16, name="x_sb")
+        ident = keep.tile([P, P], F32, name="ident")
+        ones = keep.tile([P, P], BF16, name="ones")
+        bias_rows = keep.tile([P, N], BF16, name="bias_rows")
+        bias_all = keep.tile([P, N], F32, name="bias_all")
+        grouped = keep.tile([P, GROUPS, P, PACK], BF16, name="grouped", align_bytes=64)
+        x_codes = keep.tile([P, GROUPS, P], U32, name="x_codes", align_bytes=64)
+        x_scales = keep.tile([P, GROUPS, P], U8, name="x_scales", align_bytes=64)
+        w_scales = keep.tile([P, GROUPS // PLANES, N], U8, name="w_scales", align_bytes=64)
+        w_tiles = [
+            [keep.tile([P, N * PACK], U8, name="w%d" % g, align_bytes=64)] for g in range(GROUPS - 1)
+        ]
+        w_tiles.append(
+            [
+                keep.tile([P, PIECE_COLS * PACK], U8, name="w_last%d" % piece, align_bytes=64)
+                for piece in range(LAST_PIECES)
+            ]
+        )
+        results = [keep.tile([P, PIECE_COLS], F32, name="result%d" % piece) for piece in range(LAST_PIECES)]
+
+        nc.vector.memset(w_scales[:].bitcast(I32), 0)
+        nc.vector.memset(bias_rows[:], 0.0)
+        make_identity(nc, ident[:])
+        nc.gpsimd.memset(ones[:], 1.0)
+
+        nc.sync.dma_start(out=x_sb[:], in_=x)
+        nc.scalar.dma_start(out=bias_rows[0:1, :], in_=bias.unsqueeze(0))
+        for a in range(GROUPS // PLANES):
+            for quadrant in range(QUADRANTS):
+                nc.sync.dma_start(
+                    out=w_scales[32 * quadrant : 32 * quadrant + 4 * PLANES, a, :].bitcast(I32),
+                    in_=weight_scales[
+                        PLANES * a : PLANES * (a + 1), 4 * quadrant : 4 * (quadrant + 1), :
+                    ].bitcast(I32),
+                )
+        for g in range(GROUPS):
+            pieces = len(w_tiles[g])
+            for piece in range(pieces):
+                cols = slice(piece * (N // pieces), (piece + 1) * (N // pieces))
+                nc.sync.dma_start(
+                    out=w_tiles[g][piece][:].bitcast(I32),
+                    in_=weight_words[g, :, cols, :].rearrange("p n t -> p (n t)").bitcast(I32),
+                )
+
+        x_words = x_sb[:].bitcast(F32)
+        grouped_words = grouped[:].bitcast(F32)
+        for bank in range(GROUPS // 2):
+            xt = psum.tile([P, 2, 2, P], F32, name="xt", tag="bank%d" % bank)
+            for i in range(2):
+                g = 2 * bank + i
+                for u in range(2):
+                    nc.tensor.transpose(
+                        xt[:, i, u, :], x_words[:, 256 * g + u : 256 * (g + 1) : 2], ident[:]
+                    )
+            copy = nc.vector.tensor_copy if bank % 2 == 0 else nc.scalar.copy
+            copy(
+                out=grouped_words[:, 2 * bank : 2 * bank + 2, :, :],
+                in_=xt[:].rearrange("p i u b -> p i b u"),
+            )
+        nc.vector.quantize_mx(
+            out=x_codes[:].rearrange("p g b -> p (g b)").bitcast(FP8X4),
+            scales=x_scales[:].rearrange("p g b -> p (g b)"),
+            in_=grouped[:].rearrange("p g b t -> p (g b t)"),
+        )
+
+        for bank in range(BANKS):
+            cols = slice(bank * BANK_COLS, (bank + 1) * BANK_COLS)
+            bias_ps = psum.tile([P, BANK_COLS], F32, name="bias_ps", tag="bank%d" % bank)
+            nc.tensor.matmul(out=bias_ps[:], lhsT=ones[:], rhs=bias_rows[:, cols], start=True, stop=True)
+            copy = nc.vector.tensor_copy if bank % 2 == 0 else nc.scalar.copy
+            copy(out=bias_all[:, cols], in_=bias_ps[:])
+
+        acc = [psum.tile([P, BANK_COLS], F32, name="acc%d" % bank, tag="bank%d" % bank) for bank in range(BANKS)]
+
+        def mx_pass(g, bank):
+            banks_in_tile = BANKS // len(w_tiles[g])
+            w_tile = w_tiles[g][bank // banks_in_tile]
+            first = (bank % banks_in_tile) * BANK_COLS * PACK
+            plane = PACK * (g % PLANES)
+            nc.tensor.matmul_mx(
+                out=acc[bank][:],
+                lhsT=x_codes[:, g, :].bitcast(FP8X4),
+                lhsT_scale=x_scales[:, g, :],
+                rhs=w_tile[:, first : first + BANK_COLS * PACK].bitcast(FP8X4),
+                rhs_scale=w_scales[plane:P, g // PLANES, bank * BANK_COLS : (bank + 1) * BANK_COLS],
+                start=(g == 0),
+                stop=(g == GROUPS - 1),
+            )
+
+        for g in range(GROUPS - 1):
+            for bank in range(BANKS):
+                mx_pass(g, bank)
+
+        for piece in range(LAST_PIECES):
+            piece_banks = range(piece * PIECE_BANKS, (piece + 1) * PIECE_BANKS)
+            for bank in piece_banks:
+                mx_pass(GROUPS - 1, bank)
+            for bank in piece_banks:
+                inside = (bank % PIECE_BANKS) * BANK_COLS
+                nc.vector.tensor_tensor(
+                    out=results[piece][:, inside : inside + BANK_COLS],
+                    in0=acc[bank][:],
+                    in1=bias_all[:, bank * BANK_COLS : (bank + 1) * BANK_COLS],
+                    op=mybir.AluOpType.add,
+                )
+            nc.scalar.activation(
+                out=results[piece][:], in_=results[piece][:], func=mybir.ActivationFunctionType.Relu
+            )
+            nc.sync.dma_start(
+                out=out[:, piece * PIECE_COLS : (piece + 1) * PIECE_COLS], in_=results[piece][:]
+            )

@@ -40,8 +40,8 @@ def tile_sparselinearrelu_w_kernel(tc, x, weight_words, weight_scales, bias, out
 
         x_sb = keep.tile([P, K], BF16, name="x_sb")
         ident = keep.tile([P, P], F32, name="ident")
-        ones = keep.tile([P, P], BF16, name="ones")
-        bias_rows = keep.tile([P, N], BF16, name="bias_rows")
+        ident_bf = keep.tile([P, P], BF16, name="ident_bf")
+        bias_rows = keep.tile([P, BANK_COLS], BF16, name="bias_rows")
         bias_all = keep.tile([P, N], F32, name="bias_all")
         grouped = keep.tile([P, GROUPS, P, PACK], BF16, name="grouped", align_bytes=64)
         x_codes = keep.tile([P, GROUPS, P], U32, name="x_codes", align_bytes=64)
@@ -58,13 +58,13 @@ def tile_sparselinearrelu_w_kernel(tc, x, weight_words, weight_scales, bias, out
         )
         results = [keep.tile([P, PIECE_COLS], F32, name="result%d" % piece) for piece in range(LAST_PIECES)]
 
-        nc.vector.memset(w_scales[:].bitcast(I32), 0)
         nc.vector.memset(bias_rows[:], 0.0)
+        nc.vector.memset(w_scales[:].bitcast(I32), 0)
         make_identity(nc, ident[:])
-        nc.gpsimd.memset(ones[:], 1.0)
+        make_identity(nc, ident_bf[:])
 
         nc.sync.dma_start(out=x_sb[:], in_=x)
-        nc.scalar.dma_start(out=bias_rows[0:1, :], in_=bias.unsqueeze(0))
+        nc.scalar.dma_start(out=bias_rows[0:BANKS, :], in_=bias.rearrange("(b n) -> b n", b=BANKS))
         for a in range(GROUPS // PLANES):
             for quadrant in range(QUADRANTS):
                 nc.sync.dma_start(
@@ -106,7 +106,13 @@ def tile_sparselinearrelu_w_kernel(tc, x, weight_words, weight_scales, bias, out
         for bank in range(BANKS):
             cols = slice(bank * BANK_COLS, (bank + 1) * BANK_COLS)
             bias_ps = psum.tile([P, BANK_COLS], F32, name="bias_ps", tag="bank%d" % bank)
-            nc.tensor.matmul(out=bias_ps[:], lhsT=ones[:], rhs=bias_rows[:, cols], start=True, stop=True)
+            nc.tensor.matmul(
+                out=bias_ps[:],
+                lhsT=ident_bf[:, bank : bank + 1].to_broadcast([P, P]),
+                rhs=bias_rows[:],
+                start=True,
+                stop=True,
+            )
             copy = nc.vector.tensor_copy if bank % 2 == 0 else nc.scalar.copy
             copy(out=bias_all[:, cols], in_=bias_ps[:])
 
@@ -137,15 +143,14 @@ def tile_sparselinearrelu_w_kernel(tc, x, weight_words, weight_scales, bias, out
                 mx_pass(GROUPS - 1, bank)
             for bank in piece_banks:
                 inside = (bank % PIECE_BANKS) * BANK_COLS
+                result = results[piece][:, inside : inside + BANK_COLS]
                 nc.vector.tensor_tensor(
-                    out=results[piece][:, inside : inside + BANK_COLS],
+                    out=result,
                     in0=acc[bank][:],
                     in1=bias_all[:, bank * BANK_COLS : (bank + 1) * BANK_COLS],
                     op=mybir.AluOpType.add,
                 )
-            nc.scalar.activation(
-                out=results[piece][:], in_=results[piece][:], func=mybir.ActivationFunctionType.Relu
-            )
+                nc.scalar.activation(out=result, in_=result, func=mybir.ActivationFunctionType.Relu)
             nc.sync.dma_start(
                 out=out[:, piece * PIECE_COLS : (piece + 1) * PIECE_COLS], in_=results[piece][:]
             )

@@ -20,9 +20,20 @@ BANK_COLS = 512
 BANKS = N // BANK_COLS
 PLANES = 4
 QUADRANTS = 4
-LAST_PIECES = 4
-PIECE_COLS = N // LAST_PIECES
-PIECE_BANKS = BANKS // LAST_PIECES
+LATE_FROM = 3
+EARLY_COLS = N - BANK_COLS
+PIECE_COLS = 1024
+
+
+def load_plan():
+    plan = [(g, g + 1, 0, N) for g in range(LATE_FROM)]
+    plan.extend((g, g + 1, 0, EARLY_COLS) for g in range(LATE_FROM, GROUPS - 1))
+    plan.extend(
+        (GROUPS - 1, GROUPS, c, min(c + PIECE_COLS, EARLY_COLS)) for c in range(0, EARLY_COLS, PIECE_COLS)
+    )
+    plan.append((LATE_FROM, GROUPS - 1, EARLY_COLS, N))
+    plan.append((GROUPS - 1, GROUPS, EARLY_COLS, N))
+    return plan
 
 FLOPS = 2 * P * K * N
 
@@ -47,16 +58,11 @@ def tile_sparselinearrelu_w_kernel(tc, x, weight_words, weight_scales, bias, out
         x_codes = keep.tile([P, GROUPS, P], U32, name="x_codes", align_bytes=64)
         x_scales = keep.tile([P, GROUPS, P], U8, name="x_scales", align_bytes=64)
         w_scales = keep.tile([P, GROUPS // PLANES, N], U8, name="w_scales", align_bytes=64)
+        plan = load_plan()
         w_tiles = [
-            [keep.tile([P, N * PACK], U8, name="w%d" % g, align_bytes=64)] for g in range(GROUPS - 1)
+            keep.tile([P, g1 - g0, (c1 - c0) * PACK], U8, name="w%d" % i, align_bytes=64)
+            for i, (g0, g1, c0, c1) in enumerate(plan)
         ]
-        w_tiles.append(
-            [
-                keep.tile([P, PIECE_COLS * PACK], U8, name="w_last%d" % piece, align_bytes=64)
-                for piece in range(LAST_PIECES)
-            ]
-        )
-        results = [keep.tile([P, PIECE_COLS], F32, name="result%d" % piece) for piece in range(LAST_PIECES)]
 
         nc.vector.memset(bias_rows[:], 0.0)
         nc.vector.memset(w_scales[:].bitcast(I32), 0)
@@ -73,14 +79,11 @@ def tile_sparselinearrelu_w_kernel(tc, x, weight_words, weight_scales, bias, out
                         PLANES * a : PLANES * (a + 1), 4 * quadrant : 4 * (quadrant + 1), :
                     ].bitcast(I32),
                 )
-        for g in range(GROUPS):
-            pieces = len(w_tiles[g])
-            for piece in range(pieces):
-                cols = slice(piece * (N // pieces), (piece + 1) * (N // pieces))
-                nc.sync.dma_start(
-                    out=w_tiles[g][piece][:].bitcast(I32),
-                    in_=weight_words[g, :, cols, :].rearrange("p n t -> p (n t)").bitcast(I32),
-                )
+        for i, (g0, g1, c0, c1) in enumerate(plan):
+            nc.sync.dma_start(
+                out=w_tiles[i][:].bitcast(I32),
+                in_=weight_words[g0:g1, :, c0:c1, :].rearrange("g p n t -> p g (n t)").bitcast(I32),
+            )
 
         x_words = x_sb[:].bitcast(F32)
         grouped_words = grouped[:].bitcast(F32)
@@ -118,39 +121,44 @@ def tile_sparselinearrelu_w_kernel(tc, x, weight_words, weight_scales, bias, out
 
         acc = [psum.tile([P, BANK_COLS], F32, name="acc%d" % bank, tag="bank%d" % bank) for bank in range(BANKS)]
 
-        def mx_pass(g, bank):
-            banks_in_tile = BANKS // len(w_tiles[g])
-            w_tile = w_tiles[g][bank // banks_in_tile]
-            first = (bank % banks_in_tile) * BANK_COLS * PACK
+        done = [0 for bank in range(BANKS)]
+
+        def mx_pass(i, g, bank):
+            g0, g1, c0, c1 = plan[i]
+            first = (bank * BANK_COLS - c0) * PACK
             plane = PACK * (g % PLANES)
             nc.tensor.matmul_mx(
                 out=acc[bank][:],
                 lhsT=x_codes[:, g, :].bitcast(FP8X4),
                 lhsT_scale=x_scales[:, g, :],
-                rhs=w_tile[:, first : first + BANK_COLS * PACK].bitcast(FP8X4),
+                rhs=w_tiles[i][:, g - g0, first : first + BANK_COLS * PACK].bitcast(FP8X4),
                 rhs_scale=w_scales[plane:P, g // PLANES, bank * BANK_COLS : (bank + 1) * BANK_COLS],
-                start=(g == 0),
-                stop=(g == GROUPS - 1),
+                start=(done[bank] == 0),
+                stop=(done[bank] == GROUPS - 1),
             )
+            done[bank] += 1
 
-        for g in range(GROUPS - 1):
-            for bank in range(BANKS):
-                mx_pass(g, bank)
-
-        for piece in range(LAST_PIECES):
-            piece_banks = range(piece * PIECE_BANKS, (piece + 1) * PIECE_BANKS)
-            for bank in piece_banks:
-                mx_pass(GROUPS - 1, bank)
-            for bank in piece_banks:
-                inside = (bank % PIECE_BANKS) * BANK_COLS
-                result = results[piece][:, inside : inside + BANK_COLS]
-                nc.vector.tensor_tensor(
-                    out=result,
-                    in0=acc[bank][:],
-                    in1=bias_all[:, bank * BANK_COLS : (bank + 1) * BANK_COLS],
-                    op=mybir.AluOpType.add,
-                )
-                nc.scalar.activation(out=result, in_=result, func=mybir.ActivationFunctionType.Relu)
-            nc.sync.dma_start(
-                out=out[:, piece * PIECE_COLS : (piece + 1) * PIECE_COLS], in_=results[piece][:]
-            )
+        for i, (g0, g1, c0, c1) in enumerate(plan):
+            banks = range(c0 // BANK_COLS, c1 // BANK_COLS)
+            for g in range(g0, g1):
+                for bank in banks:
+                    mx_pass(i, g, bank)
+            if done[banks[0]] < GROUPS:
+                continue
+            step = BANK_COLS // 2 if i == len(plan) - 1 else BANK_COLS
+            per_store = step if i == len(plan) - 1 else c1 - c0
+            for s0 in range(c0, c1, per_store):
+                result = keep.tile([P, per_store], F32, name="result%d_%d" % (i, s0))
+                for c in range(s0, s0 + per_store, step):
+                    nc.vector.tensor_tensor(
+                        out=result[:, c - s0 : c - s0 + step],
+                        in0=acc[c // BANK_COLS][:, c % BANK_COLS : c % BANK_COLS + step],
+                        in1=bias_all[:, c : c + step],
+                        op=mybir.AluOpType.add,
+                    )
+                    nc.scalar.activation(
+                        out=result[:, c - s0 : c - s0 + step],
+                        in_=result[:, c - s0 : c - s0 + step],
+                        func=mybir.ActivationFunctionType.Relu,
+                    )
+                nc.sync.dma_start(out=out[:, s0 : s0 + per_store], in_=result[:])

@@ -71,8 +71,8 @@ def tile_sparselinearrelu_w_kernel(tc, x, weight_words, weight_scales, bias, out
 
         nc.sync.dma_start(out=x_sb[:], in_=x)
         nc.scalar.dma_start(out=bias_rows[0:BANKS, :], in_=bias.rearrange("(b n) -> b n", b=BANKS))
-        for a in range(GROUPS // PLANES):
-            for quadrant in range(QUADRANTS):
+        for quadrant in (2, 3, 0, 1):
+            for a in range(GROUPS // PLANES):
                 nc.sync.dma_start(
                     out=w_scales[32 * quadrant : 32 * quadrant + 4 * PLANES, a, :].bitcast(I32),
                     in_=weight_scales[

@@ -20,7 +20,7 @@ BANK_COLS = 512
 BANKS = N // BANK_COLS
 PLANES = 4
 QUADRANTS = 4
-LATE_FROM = 3
+LATE_FROM = 1
 EARLY_COLS = N - BANK_COLS
 PIECE_COLS = 1024
 
@@ -31,7 +31,7 @@ def load_plan():
     plan.extend(
         (GROUPS - 1, GROUPS, c, min(c + PIECE_COLS, EARLY_COLS)) for c in range(0, EARLY_COLS, PIECE_COLS)
     )
-    plan.append((LATE_FROM, GROUPS - 1, EARLY_COLS, N))
+    plan.extend((g, g + 2, EARLY_COLS, N) for g in range(LATE_FROM, GROUPS - 1, 2))
     plan.append((GROUPS - 1, GROUPS, EARLY_COLS, N))
     return plan
 

@@ -21,13 +21,16 @@ BANKS = N // BANK_COLS
 PLANES = 4
 QUADRANTS = 4
 LATE_FROM = 1
+PAIRS_TO = 5
 EARLY_COLS = N - BANK_COLS
-PIECE_COLS = 1024
+PIECE_COLS = 2048
+STORE_COLS = 1024
 
 
 def load_plan():
     plan = [(g, g + 1, 0, N) for g in range(LATE_FROM)]
-    plan.extend((g, g + 1, 0, EARLY_COLS) for g in range(LATE_FROM, GROUPS - 1))
+    plan.extend((g, g + 2, 0, EARLY_COLS) for g in range(LATE_FROM, PAIRS_TO, 2))
+    plan.extend((g, g + 1, 0, EARLY_COLS) for g in range(PAIRS_TO, GROUPS - 1))
     plan.extend(
         (GROUPS - 1, GROUPS, c, min(c + PIECE_COLS, EARLY_COLS)) for c in range(0, EARLY_COLS, PIECE_COLS)
     )
@@ -146,8 +149,8 @@ def tile_sparselinearrelu_w_kernel(tc, x, weight_words, weight_scales, bias, out
             if done[banks[0]] < GROUPS:
                 continue
             step = BANK_COLS // 2 if i == len(plan) - 1 else BANK_COLS
-            per_store = step if i == len(plan) - 1 else c1 - c0
-            for s0 in range(c0, c1, per_store):
+            for s0 in range(c0, c1, step if i == len(plan) - 1 else STORE_COLS):
+                per_store = step if i == len(plan) - 1 else min(STORE_COLS, c1 - s0)
                 result = keep.tile([P, per_store], F32, name="result%d_%d" % (i, s0))
                 for c in range(s0, s0 + per_store, step):
                     nc.vector.tensor_tensor(

@@ -24,7 +24,6 @@ LATE_FROM = 1
 PAIRS_TO = 5
 EARLY_COLS = N - BANK_COLS
 PIECE_COLS = 2048
-STORE_COLS = 1024
 
 
 def load_plan():
@@ -149,19 +148,17 @@ def tile_sparselinearrelu_w_kernel(tc, x, weight_words, weight_scales, bias, out
             if done[banks[0]] < GROUPS:
                 continue
             step = BANK_COLS // 2 if i == len(plan) - 1 else BANK_COLS
-            for s0 in range(c0, c1, step if i == len(plan) - 1 else STORE_COLS):
-                per_store = step if i == len(plan) - 1 else min(STORE_COLS, c1 - s0)
-                result = keep.tile([P, per_store], F32, name="result%d_%d" % (i, s0))
-                for c in range(s0, s0 + per_store, step):
-                    nc.vector.tensor_tensor(
-                        out=result[:, c - s0 : c - s0 + step],
-                        in0=acc[c // BANK_COLS][:, c % BANK_COLS : c % BANK_COLS + step],
-                        in1=bias_all[:, c : c + step],
-                        op=mybir.AluOpType.add,
-                    )
-                    nc.scalar.activation(
-                        out=result[:, c - s0 : c - s0 + step],
-                        in_=result[:, c - s0 : c - s0 + step],
-                        func=mybir.ActivationFunctionType.Relu,
-                    )
-                nc.sync.dma_start(out=out[:, s0 : s0 + per_store], in_=result[:])
+            result = keep.tile([P, c1 - c0], F32, name="result%d" % i)
+            for c in range(c0, c1, step):
+                nc.vector.tensor_tensor(
+                    out=result[:, c - c0 : c - c0 + step],
+                    in0=acc[c // BANK_COLS][:, c % BANK_COLS : c % BANK_COLS + step],
+                    in1=bias_all[:, c : c + step],
+                    op=mybir.AluOpType.add,
+                )
+                nc.scalar.activation(
+                    out=result[:, c - c0 : c - c0 + step],
+                    in_=result[:, c - c0 : c - c0 + step],
+                    func=mybir.ActivationFunctionType.Relu,
+                )
+            nc.sync.dma_start(out=out[:, c0:c1], in_=result[:])

from contextlib import ExitStack

import concourse.mybir as mybir
from concourse.masks import make_identity

BF16 = mybir.dt.bfloat16
F32 = mybir.dt.float32
I32 = mybir.dt.int32
U8 = mybir.dt.uint8
U32 = mybir.dt.uint32
FP8X4 = mybir.dt.float8_e4m3fn_x4

P = 128
PACK = 4
K_PASS = P * PACK
K = 4096
N = 4096
GROUPS = K // K_PASS
BANK_COLS = 512
BANKS = N // BANK_COLS
PLANES = 4
QUADRANTS = 4
LATE_FROM = 1
PAIRS_TO = 5
EARLY_COLS = N - BANK_COLS
PIECE_COLS = 2048


def load_plan():
    plan = [(g, g + 1, 0, N) for g in range(LATE_FROM)]
    plan.extend((g, g + 2, 0, EARLY_COLS) for g in range(LATE_FROM, PAIRS_TO, 2))
    plan.extend((g, g + 1, 0, EARLY_COLS) for g in range(PAIRS_TO, GROUPS - 1))
    plan.extend(
        (GROUPS - 1, GROUPS, c, min(c + PIECE_COLS, EARLY_COLS)) for c in range(0, EARLY_COLS, PIECE_COLS)
    )
    plan.extend((g, g + 2, EARLY_COLS, N) for g in range(LATE_FROM, GROUPS - 1, 2))
    plan.append((GROUPS - 1, GROUPS, EARLY_COLS, N))
    return plan

FLOPS = 2 * P * K * N


def tile_sparselinearrelu_w_kernel(tc, x, weight_words, weight_scales, bias, out):
    nc = tc.nc
    assert tuple(x.shape) == (P, K)
    assert tuple(weight_words.shape) == (GROUPS, P, N, PACK)
    assert tuple(weight_scales.shape) == (GROUPS, K_PASS // 32, N)

    with ExitStack() as ctx:
        keep = ctx.enter_context(tc.tile_pool(name="keep", bufs=1))
        psum = ctx.enter_context(tc.psum_pool(name="psum", bufs=1))
        ctx.enter_context(tc.manual_schedule())

        x_sb = keep.tile([P, K], BF16, name="x_sb")
        ident = keep.tile([P, P], F32, name="ident")
        ident_bf = keep.tile([P, P], BF16, name="ident_bf")
        bias_rows = keep.tile([P, BANK_COLS], BF16, name="bias_rows")
        bias_all = keep.tile([P, N], F32, name="bias_all")
        grouped = keep.tile([P, GROUPS, P, PACK], BF16, name="grouped", align_bytes=64)
        x_codes = keep.tile([P, GROUPS, P], U32, name="x_codes", align_bytes=64)
        x_scales = keep.tile([P, GROUPS, P], U8, name="x_scales", align_bytes=64)
        w_scales = keep.tile([P, GROUPS // PLANES, N], U8, name="w_scales", align_bytes=64)
        plan = load_plan()
        w_tiles = [
            keep.tile([P, g1 - g0, (c1 - c0) * PACK], U8, name="w%d" % i, align_bytes=64)
            for i, (g0, g1, c0, c1) in enumerate(plan)
        ]

        nc.vector.memset(bias_rows[:], 0.0)
        nc.vector.memset(w_scales[:].bitcast(I32), 0)
        make_identity(nc, ident[:])
        make_identity(nc, ident_bf[:])

        nc.sync.dma_start(out=x_sb[:], in_=x)
        nc.scalar.dma_start(out=bias_rows[0:BANKS, :], in_=bias.rearrange("(b n) -> b n", b=BANKS))
        for quadrant in (2, 3, 0, 1):
            for a in range(GROUPS // PLANES):
                nc.sync.dma_start(
                    out=w_scales[32 * quadrant : 32 * quadrant + 4 * PLANES, a, :].bitcast(I32),
                    in_=weight_scales[
                        PLANES * a : PLANES * (a + 1), 4 * quadrant : 4 * (quadrant + 1), :
                    ].bitcast(I32),
                )
        for i, (g0, g1, c0, c1) in enumerate(plan):
            nc.sync.dma_start(
                out=w_tiles[i][:].bitcast(I32),
                in_=weight_words[g0:g1, :, c0:c1, :].rearrange("g p n t -> p g (n t)").bitcast(I32),
            )

        x_words = x_sb[:].bitcast(F32)
        grouped_words = grouped[:].bitcast(F32)
        for bank in range(GROUPS // 2):
            xt = psum.tile([P, 2, 2, P], F32, name="xt", tag="bank%d" % bank)
            for i in range(2):
                g = 2 * bank + i
                for u in range(2):
                    nc.tensor.transpose(
                        xt[:, i, u, :], x_words[:, 256 * g + u : 256 * (g + 1) : 2], ident[:]
                    )
            copy = nc.vector.tensor_copy if bank % 2 == 0 else nc.scalar.copy
            copy(
                out=grouped_words[:, 2 * bank : 2 * bank + 2, :, :],
                in_=xt[:].rearrange("p i u b -> p i b u"),
            )
        nc.vector.quantize_mx(
            out=x_codes[:].rearrange("p g b -> p (g b)").bitcast(FP8X4),
            scales=x_scales[:].rearrange("p g b -> p (g b)"),
            in_=grouped[:].rearrange("p g b t -> p (g b t)"),
        )

        for bank in range(BANKS):
            cols = slice(bank * BANK_COLS, (bank + 1) * BANK_COLS)
            bias_ps = psum.tile([P, BANK_COLS], F32, name="bias_ps", tag="bank%d" % bank)
            nc.tensor.matmul(
                out=bias_ps[:],
                lhsT=ident_bf[:, bank : bank + 1].to_broadcast([P, P]),
                rhs=bias_rows[:],
                start=True,
                stop=True,
            )
            copy = nc.vector.tensor_copy if bank % 2 == 0 else nc.scalar.copy
            copy(out=bias_all[:, cols], in_=bias_ps[:])

        acc = [psum.tile([P, BANK_COLS], F32, name="acc%d" % bank, tag="bank%d" % bank) for bank in range(BANKS)]

        done = [0 for bank in range(BANKS)]

        def mx_pass(i, g, bank):
            g0, g1, c0, c1 = plan[i]
            first = (bank * BANK_COLS - c0) * PACK
            plane = PACK * (g % PLANES)
            nc.tensor.matmul_mx(
                out=acc[bank][:],
                lhsT=x_codes[:, g, :].bitcast(FP8X4),
                lhsT_scale=x_scales[:, g, :],
                rhs=w_tiles[i][:, g - g0, first : first + BANK_COLS * PACK].bitcast(FP8X4),
                rhs_scale=w_scales[plane:P, g // PLANES, bank * BANK_COLS : (bank + 1) * BANK_COLS],
                start=(done[bank] == 0),
                stop=(done[bank] == GROUPS - 1),
            )
            done[bank] += 1

        for i, (g0, g1, c0, c1) in enumerate(plan):
            banks = range(c0 // BANK_COLS, c1 // BANK_COLS)
            for g in range(g0, g1):
                for bank in banks:
                    mx_pass(i, g, bank)
            if done[banks[0]] < GROUPS:
                continue
            step = BANK_COLS // 2 if i == len(plan) - 1 else BANK_COLS
            result = keep.tile([P, c1 - c0], F32, name="result%d" % i)
            for c in range(c0, c1, step):
                nc.vector.tensor_tensor(
                    out=result[:, c - c0 : c - c0 + step],
                    in0=acc[c // BANK_COLS][:, c % BANK_COLS : c % BANK_COLS + step],
                    in1=bias_all[:, c : c + step],
                    op=mybir.AluOpType.add,
                )
                nc.scalar.activation(
                    out=result[:, c - c0 : c - c0 + step],
                    in_=result[:, c - c0 : c - c0 + step],
                    func=mybir.ActivationFunctionType.Relu,
                )
            nc.sync.dma_start(out=out[:, c0:c1], in_=result[:])
